import numpy as np
import ml_dtypes


def mxq(x, axis, fmt="e4m3"):
    dtype, down = {"e4m3": (ml_dtypes.float8_e4m3fn, 7), "e5m2": (ml_dtypes.float8_e5m2, 14)}[fmt]
    v = np.moveaxis(np.asarray(x, np.float32).astype(ml_dtypes.bfloat16).astype(np.float64), axis, -1)
    blocks = v.reshape(v.shape[:-1] + (-1, 32))
    amax = np.abs(blocks).max(-1, keepdims=True)
    byte = np.maximum(np.where(amax > 0, np.frexp(amax)[1] - 1 + 127, 0) - down, 1)
    scale = np.exp2(byte - 127.0)
    codes = (blocks / scale).astype(np.float32).astype(dtype).astype(np.float64)
    return np.moveaxis((codes * scale).reshape(v.shape), -1, axis)


WIDE = False


def mx_kscale(k):
    if not WIDE:
        return np.ones(k)
    levels = np.array([30, -30])
    if k % 512:
        return np.exp2(np.random.permutation(np.resize(levels, k // 32))).repeat(32)
    a = np.empty((k // 512, 16))
    for p in range(k // 512):
        a[p, :8] = np.random.permutation(np.resize(levels, 8))
        for g in range(8):
            far = levels[np.abs(levels - a[p, g]) >= 10]
            a[p, g + 8] = far[np.random.randint(len(far))]
    return np.exp2(a.ravel()).repeat(32)


BF16 = ml_dtypes.bfloat16


def bf(x):
    return np.asarray(x, np.float32).astype(BF16)


def f64(x):
    return np.asarray(x).astype(np.float64)


E2M1 = np.array([0.0, 0.5, 1.0, 1.5, 2.0, 3.0, 4.0, 6.0, -0.0, -0.5, -1.0, -1.5, -2.0, -3.0, -4.0, -6.0])


def pack_weight(w, fmt):
    k, n = w.shape
    w = f64(bf(w)).reshape(k // 32, 32, n)
    amax = np.abs(w).max(1)
    if fmt == "e4m3":
        byte = np.frexp(amax)[1] - 1 + 127 - 7
    else:
        mant, ex = np.frexp(amax / 6.0)
        byte = np.where(mant > 0.5, ex, ex - 1) + 127
    byte = np.clip(np.where(amax > 0, byte, 1), 1, 254)
    scaled = (w * np.exp2(127.0 - byte)[:, None, :]).reshape(k, n).astype(np.float32)
    by_word = np.ascontiguousarray(scaled.reshape(k // 512, 128, 4, n).transpose(0, 1, 3, 2))
    if fmt == "e4m3":
        words = by_word.astype(ml_dtypes.float8_e4m3fn).view(np.uint8)
    else:
        c = by_word.astype(ml_dtypes.float4_e2m1fn).view(np.uint8) & 0xF
        words = c[..., 0::2] | (c[..., 1::2] << 4)
    return np.ascontiguousarray(words), np.ascontiguousarray(byte.astype(np.uint8).reshape(k // 512, 16, n))


def unpack_weight(words, scales, fmt):
    g, p, n, _ = words.shape
    if fmt == "e4m3":
        vals = np.ascontiguousarray(words).view(ml_dtypes.float8_e4m3fn).astype(np.float64)
    else:
        nib = np.empty((g, p, n, 4), np.uint8)
        nib[..., 0::2] = words & 0xF
        nib[..., 1::2] = words >> 4
        vals = E2M1[nib]
    vals = vals * np.repeat(np.exp2(scales.astype(np.float64) - 127.0), 8, axis=1)[..., None]
    return vals.transpose(0, 1, 3, 2).reshape(g * 512, n)

def pack4(w):
    words, scales = pack_weight(w, "e2m1")
    return words.reshape(words.shape[0], 128, -1), scales


def unpack4(words, scales):
    return unpack_weight(words.reshape(words.shape[0], 128, -1, 2), scales, "e2m1")


B, C, E, H, HS, WS = 2, 512, 1536, 16, 32, 32
N = HS * WS
EPS = 1e-5
A = 2.0 * (E / H) ** -0.5 / np.sqrt(N)


def chan_layernorm(x, g):
    mean = x.mean(axis=1, keepdims=True)
    var = x.var(axis=1, keepdims=True)
    return (x - mean) * (1.0 / np.sqrt(var + EPS)) * g


def setup_inputs():
    s = mx_kscale(E)
    h_attn = bf(np.random.standard_normal((B, E, HS, WS)) * A * s[None, :, None, None])
    xn = bf(np.random.standard_normal((B, C, HS, WS)))
    wout = np.random.standard_normal((C, E)) / (np.sqrt(E) * A) / s[None, :]
    words, scales = pack4(np.ascontiguousarray(wout.T))
    bout = bf(0.3 * np.random.standard_normal(C))
    outnorm_g = bf(1.0 + 0.1 * np.random.standard_normal((1, C, 1, 1)))
    return {"h_attn": h_attn,
            "xn": xn,
            "Wout_words": words,
            "Wout_scales": scales,
            "bout": bout,
            "outnorm_g": outnorm_g}


def reference(h_attn, xn, Wout_words, Wout_scales, bout, outnorm_g):
    a = f64(h_attn).reshape(B, E, N)
    y = (unpack4(Wout_words, Wout_scales).T @ mxq(a, 1, "e5m2")) + f64(bout)[None, :, None]
    y = y.reshape(B, C, HS, WS)
    return chan_layernorm(y, f64(outnorm_g)) + f64(xn)

@@ -1,0 +1,255 @@
+from contextlib import ExitStack
+
+import concourse.mybir as mybir
+from concourse.masks import make_identity
+
+B, C, E, N = 2, 512, 1536, 1024
+EPS = 1e-5
+FLOPS = 2 * B * C * E * N
+
+F32 = mybir.dt.float32
+BF16 = mybir.dt.bfloat16
+U32 = mybir.dt.uint32
+I32 = mybir.dt.int32
+U8 = mybir.dt.uint8
+E5M2X4 = mybir.dt.float8_e5m2_x4
+E2M1X4 = mybir.dt.float4_e2m1fn_x4
+ALU = mybir.AluOpType
+ACT = mybir.ActivationFunctionType
+
+P = 128
+PACK = 4
+PASSES = E // (P * PACK)
+TILE = 128
+CH = C // P
+H_RANGES = [(0, 256),(256, 512),(512, 1024),(1024, 1536),(1536, 2048)]
+XN_RANGES = [(0, 512), (512, 1024), (1024, 1536), (1536, 2048)]
+UNITS = [(0, 256), (256, 512), (512, 768), (768, 1024), (1024, 1280), (1280, 1536), (1536, 1792), (1792, 1920), (1920, 2048)]
+
+
+def tile_linearattention_pb_kernel(tc, h_attn, xn, Wout_words, Wout_scales, bout, outnorm_g, out):
+    nc = tc.nc
+    h_v = h_attn.rearrange("b (g p j) y x -> b g p j (y x)", p=P, j=PACK)
+    xn_v = xn.rearrange("b (p j) y x -> b p j (y x)", j=CH)
+    out_v = out.rearrange("b (p j) y x -> b p j (y x)", j=CH)
+
+    with ExitStack() as ctx:
+        keep = ctx.enter_context(tc.tile_pool(name="keep", bufs=1))
+        work = ctx.enter_context(tc.tile_pool(name="work", bufs=4))
+        acc_pool = ctx.enter_context(tc.psum_pool(name="acc", bufs=4))
+        tr_pool = ctx.enter_context(tc.psum_pool(name="tr", bufs=4))
+        ctx.enter_context(tc.manual_schedule())
+
+        raw, res = {}, {}
+
+        def load_h(r):
+            lo, hi = H_RANGES[r]
+            for g in range(PASSES):
+                t = keep.tile([P, PACK, hi - lo], BF16, name="raw_%d_%d" % (r, g))
+                nc.sync.dma_start(out=t[:], in_=h_v[lo // N, g, :, :, lo % N : lo % N + hi - lo])
+                for u, (a, b) in enumerate(UNITS):
+                    if lo <= a < hi:
+                        raw[u, g] = t[:, :, a - lo : b - lo]
+
+        def load_xn(r):
+            lo, hi = XN_RANGES[r]
+            t = keep.tile([P, CH, hi - lo], BF16, name="xn_%d" % r)
+            nc.sync.dma_start(out=t[:], in_=xn_v[lo // N, :, :, lo % N : lo % N + hi - lo])
+            for u, (a, b) in enumerate(UNITS):
+                if lo <= a < hi:
+                    res[u] = t[:, :, a - lo : b - lo]
+
+        words = keep.tile([P, PASSES, 2 * C], U8, name="words", align_bytes=64)
+        w_scale = keep.tile([P, PASSES, C], U8, name="w_scale", align_bytes=64)
+        bias4 = keep.tile([P, CH], BF16, name="bias4")
+        gain4 = keep.tile([P, CH], BF16, name="gain4")
+        nc.scalar.dma_start(out=bias4[:], in_=bout.rearrange("(p j) -> p j", j=CH))
+        nc.scalar.dma_start(out=gain4[:], in_=outnorm_g.rearrange("o (p j) y x -> p (o j y x)", j=CH))
+        for q in range(4):
+            nc.gpsimd.dma_start(
+                out=w_scale[32 * q : 32 * q + 4, :, :].bitcast(I32),
+                in_=Wout_scales[:, 4 * q : 4 * q + 4, :].rearrange("g r n -> r g n").bitcast(I32),
+            )
+
+        load_h(0)
+        nc.sync.dma_start(out=words[:].bitcast(I32), in_=Wout_words.rearrange("g p n -> p g n").bitcast(I32))
+        load_h(1)
+        load_h(2)
+        load_xn(0)
+        load_h(3)
+        load_xn(1)
+        load_h(4)
+        load_xn(2)
+        load_xn(3)
+
+        ident = keep.tile([P, P], F32, name="ident")
+        make_identity(nc, ident[:])
+        bias4f = keep.tile([P, CH], F32, name="bias4f")
+        nc.scalar.activation(out=bias4f[:], in_=bias4[:], func=ACT.Copy)
+        bias_ps = tr_pool.tile([P, C], F32, name="bias_ps", tag="tr")
+        for j in range(CH):
+            nc.tensor.transpose(bias_ps[:, j * P : (j + 1) * P], bias4f[:, j : j + 1].to_broadcast([P, P]), ident[:])
+        bias_all = keep.tile([P, C], F32, name="bias_all")
+
+        grouped, codes, scales, acc, y, z, total, sumsq, rstd, nmean, zt = ({} for k in range(11))
+
+        def tiles(u):
+            return range((UNITS[u][1] - UNITS[u][0]) // TILE) if 0 <= u < len(UNITS) else range(0)
+
+        def on_vector(u, g):
+            return (u == 0 and g != 1) or (0 < u < 3 and g > 0) or (g == 2 and u < 7)
+
+        def interleave(u, g, vector):
+            if not tiles(u) or on_vector(u, g) != vector:
+                return
+            t = work.tile([P, len(tiles(u)) * TILE, PACK], BF16, name="grouped", tag="grouped", bufs=7, align_bytes=64)
+            grouped[u, g] = t
+            dst = t[:].rearrange("p (c i) t -> p c t i", i=4)
+            src = raw[u, g].rearrange("p t (c i) -> p c t i", i=4)
+            if vector:
+                nc.vector.tensor_copy(out=dst, in_=src)
+            else:
+                nc.scalar.copy(out=dst, in_=src)
+
+        def quantise(u, g):
+            if not tiles(u):
+                return
+            width = len(tiles(u)) * TILE
+            cd = work.tile([P, width], U32, name="codes", tag="codes", bufs=9, align_bytes=64)
+            sc = work.tile([P, width], U8, name="scales", tag="scales", bufs=9, align_bytes=64)
+            codes[u, g], scales[u, g] = cd, sc
+            nc.vector.quantize_mx(
+                out=cd[:].bitcast(E5M2X4), scales=sc[:], in_=grouped[u, g][:].rearrange("p n t -> p (n t)")
+            )
+
+        def multiply(u, i):
+            if i not in tiles(u):
+                return
+            a = acc_pool.tile([P, C], F32, name="acc", tag="acc")
+            acc[u, i] = a
+            cols = slice(i * TILE, (i + 1) * TILE)
+            for g in range(PASSES):
+                nc.tensor.matmul_mx(
+                    out=a[:],
+                    lhsT=codes[u, g][:, cols].bitcast(E5M2X4),
+                    lhsT_scale=scales[u, g][:, cols],
+                    rhs=words[:, g, :].bitcast(E2M1X4),
+                    rhs_scale=w_scale[:, g, :],
+                    start=(g == 0),
+                    stop=(g == PASSES - 1),
+                )
+
+        def add_bias(u, i):
+            if i in tiles(u):
+                if i == 0:
+                    total[u] = work.tile([P, len(tiles(u))], F32, name="total", tag="total")
+                y[u, i] = work.tile([P, C], F32, name="y", tag="y", bufs=6)
+                nc.vector.scalar_tensor_tensor(
+                    out=y[u, i][:].rearrange("n (j p) -> n j p", j=CH),
+                    in0=acc[u, i][:].rearrange("n (p j) -> n j p", j=CH),
+                    scalar=1.0,
+                    in1=bias_all[:].rearrange("n (j p) -> n j p", j=CH),
+                    op0=ALU.mult,
+                    op1=ALU.add,
+                    accum_out=total[u][:, i : i + 1],
+                )
+
+        def negate_mean(u, i):
+            if i not in tiles(u):
+                return
+            nmean[u, i] = work.tile([P, 1], F32, name="nmean", tag="nmean", bufs=8)
+            nc.gpsimd.tensor_scalar(
+                out=nmean[u, i][:], in0=total[u][:, i : i + 1], scalar1=-1.0 / C, scalar2=0.0, op0=ALU.mult, op1=ALU.add
+            )
+
+        def variance(u, i):
+            if i in tiles(u):
+                if i == 0:
+                    sumsq[u] = work.tile([P, len(tiles(u))], F32, name="sumsq", tag="sumsq")
+                squares = work.tile([P, C], BF16, name="squares", tag="squares", bufs=2)
+                nc.scalar.activation(
+                    out=squares[:],
+                    in_=y[u, i][:],
+                    func=ACT.Square,
+                    bias=total[u][:, i : i + 1],
+                    scale=-float(C),
+                    accum_out=sumsq[u][:, i : i + 1],
+                )
+
+        def inverse_std(u):
+            if not tiles(u):
+                return
+            rstd[u] = work.tile([P, len(tiles(u))], F32, name="rstd", tag="rstd")
+            nc.scalar.activation(
+                out=rstd[u][:], in_=sumsq[u][:], func=ACT.Abs_reciprocal_sqrt, bias=EPS, scale=1.0 / C**3
+            )
+
+        def normalise(u, i):
+            if i in tiles(u):
+                z[u, i] = work.tile([P, C], F32, name="z", tag="z", bufs=4)
+                eng = nc.gpsimd
+                eng.tensor_scalar(
+                    out=z[u, i][:],
+                    in0=y[u, i][:],
+                    scalar1=nmean[u, i][:],
+                    scalar2=rstd[u][:, i : i + 1],
+                    op0=ALU.add,
+                    op1=ALU.mult,
+                )
+
+        def transpose(u, i):
+            if i not in tiles(u):
+                return
+            n = len(tiles(u))
+            if i == 0:
+                for k in range(n):
+                    bank = tr_pool.tile([P, C], F32, name="zt", tag="tr")
+                    for j in range(CH // n):
+                        zt[u, k * (CH // n) + j] = bank[:, j * n * TILE : (j + 1) * n * TILE]
+            for j in range(CH):
+                nc.tensor.transpose(zt[u, j][:, i * TILE : (i + 1) * TILE], z[u, i][:, j * P : (j + 1) * P], ident[:])
+
+        def finish(u):
+            if not tiles(u):
+                return
+            lo, hi = UNITS[u]
+            o = keep.tile([P, CH, hi - lo], F32, name="out_%d" % u)
+            for j in range(CH):
+                nc.vector.scalar_tensor_tensor(
+                    out=o[:, j, :],
+                    in0=zt[u, j],
+                    scalar=gain4[:, j : j + 1],
+                    in1=res[u][:, j, :],
+                    op0=ALU.mult,
+                    op1=ALU.add,
+                )
+            nc.sync.dma_start(out=out_v[lo // N, :, :, lo % N : lo % N + hi - lo], in_=o[:])
+
+        for g in range(PASSES):
+            interleave(0, g, False)
+        for s in range(len(UNITS) + 3):
+            variance(s - 2, 0)
+            variance(s - 2, 1)
+            interleave(s + 1, 0, False)
+            inverse_std(s - 2)
+            interleave(s, 0, True)
+            interleave(s, 1, True)
+            quantise(s, 0)
+            interleave(s, 2, True)
+            quantise(s, 1)
+            quantise(s, 2)
+            if s == 0:
+                nc.scalar.copy(out=bias_all[:], in_=bias_ps[:])
+            multiply(s, 0)
+            add_bias(s - 1, 0)
+            negate_mean(s - 1, 0)
+            add_bias(s - 1, 1)
+            interleave(s + 1, 1, False)
+            interleave(s + 1, 2, False)
+            finish(s - 3)
+            normalise(s - 2, 0)
+            normalise(s - 2, 1)
+            negate_mean(s - 1, 1)
+            transpose(s - 2, 0)
+            multiply(s, 1)
+            transpose(s - 2, 1)

@@ -63,10 +63,9 @@ def tile_linearattention_pb_kernel(tc, h_attn, xn, Wout_words, Wout_scales, bout
         w_scale = keep.tile([P, PASSES, C], U8, name="w_scale", align_bytes=64)
         bias4 = keep.tile([P, CH], BF16, name="bias4")
         gain4 = keep.tile([P, CH], BF16, name="gain4")
-        nc.scalar.dma_start(out=bias4[:], in_=bout.rearrange("(p j) -> p j", j=CH))
-        nc.scalar.dma_start(out=gain4[:], in_=outnorm_g.rearrange("o (p j) y x -> p (o j y x)", j=CH))
+        nc.gpsimd.dma_start(out=bias4[:], in_=bout.rearrange("(p j) -> p j", j=CH))
         for q in range(4):
-            nc.gpsimd.dma_start(
+            nc.scalar.dma_start(
                 out=w_scale[32 * q : 32 * q + 4, :, :].bitcast(I32),
                 in_=Wout_scales[:, 4 * q : 4 * q + 4, :].rearrange("g r n -> r g n").bitcast(I32),
             )
@@ -84,6 +83,7 @@ def tile_linearattention_pb_kernel(tc, h_attn, xn, Wout_words, Wout_scales, bout
 
         ident = keep.tile([P, P], F32, name="ident")
         make_identity(nc, ident[:])
+        nc.gpsimd.dma_start(out=gain4[:], in_=outnorm_g.rearrange("o (p j) y x -> p (o j y x)", j=CH))
         bias4f = keep.tile([P, CH], F32, name="bias4f")
         nc.scalar.activation(out=bias4f[:], in_=bias4[:], func=ACT.Copy)
         bias_ps = tr_pool.tile([P, C], F32, name="bias_ps", tag="tr")
@@ -227,6 +227,7 @@ def tile_linearattention_pb_kernel(tc, h_attn, xn, Wout_words, Wout_scales, bout
 
         for g in range(PASSES):
             interleave(0, g, False)
+        nc.scalar.copy(out=bias_all[:], in_=bias_ps[:])
         for s in range(len(UNITS) + 3):
             variance(s - 2, 0)
             variance(s - 2, 1)
@@ -238,8 +239,6 @@ def tile_linearattention_pb_kernel(tc, h_attn, xn, Wout_words, Wout_scales, bout
             interleave(s, 2, True)
             quantise(s, 1)
             quantise(s, 2)
-            if s == 0:
-                nc.scalar.copy(out=bias_all[:], in_=bias_ps[:])
             multiply(s, 0)
             add_bias(s - 1, 0)
             negate_mean(s - 1, 0)

@@ -22,9 +22,11 @@ PACK = 4
 PASSES = E // (P * PACK)
 TILE = 128
 CH = C // P
-H_RANGES = [(0, 256),(256, 512),(512, 1024),(1024, 1536),(1536, 2048)]
-XN_RANGES = [(0, 512), (512, 1024), (1024, 1536), (1536, 2048)]
+H_RANGES = [(0, 256), (256, 512), (512, 1024), (1024, 2048)]
+XN_RANGES = [(0, 512), (512, 1024), (1024, 2048)]
 UNITS = [(0, 256), (256, 512), (512, 768), (768, 1024), (1024, 1280), (1280, 1536), (1536, 1792), (1792, 1920), (1920, 2048)]
+STORES = [(0, 1), (2, 3), (4, 4), (5, 5), (6, 6), (7, 7), (8, 8)]
+NORM_ON_SCALAR = 7
 
 
 def tile_linearattention_pb_kernel(tc, h_attn, xn, Wout_words, Wout_scales, bout, outnorm_g, out):
@@ -40,11 +42,11 @@ def tile_linearattention_pb_kernel(tc, h_attn, xn, Wout_words, Wout_scales, bout
         tr_pool = ctx.enter_context(tc.psum_pool(name="tr", bufs=4))
         ctx.enter_context(tc.manual_schedule())
 
-        raw, res = {}, {}
+        raw, res, outs = {}, {}, {}
 
-        def load_h(r):
+        def load_h(r, passes=range(PASSES)):
             lo, hi = H_RANGES[r]
-            for g in range(PASSES):
+            for g in passes:
                 t = keep.tile([P, PACK, hi - lo], BF16, name="raw_%d_%d" % (r, g))
                 nc.sync.dma_start(out=t[:], in_=h_v[lo // N, g, :, :, lo % N : lo % N + hi - lo])
                 for u, (a, b) in enumerate(UNITS):
@@ -74,12 +76,11 @@ def tile_linearattention_pb_kernel(tc, h_attn, xn, Wout_words, Wout_scales, bout
         nc.sync.dma_start(out=words[:].bitcast(I32), in_=Wout_words.rearrange("g p n -> p g n").bitcast(I32))
         load_h(1)
         load_h(2)
+        load_h(3, [0])
         load_xn(0)
-        load_h(3)
+        load_h(3, [1, 2])
         load_xn(1)
-        load_h(4)
         load_xn(2)
-        load_xn(3)
 
         ident = keep.tile([P, P], F32, name="ident")
         make_identity(nc, ident[:])
@@ -96,16 +97,24 @@ def tile_linearattention_pb_kernel(tc, h_attn, xn, Wout_words, Wout_scales, bout
         def tiles(u):
             return range((UNITS[u][1] - UNITS[u][0]) // TILE) if 0 <= u < len(UNITS) else range(0)
 
-        def on_vector(u, g):
-            return (u == 0 and g != 1) or (0 < u < 3 and g > 0) or (g == 2 and u < 7)
+        def vector_columns(u, g):
+            width = UNITS[u][1] - UNITS[u][0]
+            return width if (u == 0 and g != 1) or (0 < u < 3 and g > 0) else (width * 5 // 8 if g == 2 and u < 7 else 0)
 
         def interleave(u, g, vector):
-            if not tiles(u) or on_vector(u, g) != vector:
+            if not tiles(u):
                 return
-            t = work.tile([P, len(tiles(u)) * TILE, PACK], BF16, name="grouped", tag="grouped", bufs=7, align_bytes=64)
-            grouped[u, g] = t
-            dst = t[:].rearrange("p (c i) t -> p c t i", i=4)
-            src = raw[u, g].rearrange("p t (c i) -> p c t i", i=4)
+            width = UNITS[u][1] - UNITS[u][0]
+            cut = width - vector_columns(u, g)
+            cols = slice(cut, width) if vector else slice(0, cut)
+            if cols.start == cols.stop:
+                return
+            if (u, g) not in grouped:
+                grouped[u, g] = work.tile(
+                    [P, width, PACK], BF16, name="grouped", tag="grouped", bufs=7, align_bytes=64
+                )
+            dst = grouped[u, g][:, cols, :].rearrange("p (c i) t -> p c t i", i=4)
+            src = raw[u, g][:, :, cols].rearrange("p t (c i) -> p c t i", i=4)
             if vector:
                 nc.vector.tensor_copy(out=dst, in_=src)
             else:
@@ -122,15 +131,13 @@ def tile_linearattention_pb_kernel(tc, h_attn, xn, Wout_words, Wout_scales, bout
                 out=cd[:].bitcast(E5M2X4), scales=sc[:], in_=grouped[u, g][:].rearrange("p n t -> p (n t)")
             )
 
-        def multiply(u, i):
-            if i not in tiles(u):
-                return
-            a = acc_pool.tile([P, C], F32, name="acc", tag="acc")
-            acc[u, i] = a
-            cols = slice(i * TILE, (i + 1) * TILE)
-            for g in range(PASSES):
+        def multiply(u, g):
+            for i in tiles(u):
+                if g == 0:
+                    acc[u, i] = acc_pool.tile([P, C], F32, name="acc", tag="acc")
+                cols = slice(i * TILE, (i + 1) * TILE)
                 nc.tensor.matmul_mx(
-                    out=a[:],
+                    out=acc[u, i][:],
                     lhsT=codes[u, g][:, cols].bitcast(E5M2X4),
                     lhsT_scale=scales[u, g][:, cols],
                     rhs=words[:, g, :].bitcast(E2M1X4),
@@ -154,13 +161,11 @@ def tile_linearattention_pb_kernel(tc, h_attn, xn, Wout_words, Wout_scales, bout
                     accum_out=total[u][:, i : i + 1],
                 )
 
-        def negate_mean(u, i):
-            if i not in tiles(u):
+        def negate_mean(u):
+            if not tiles(u):
                 return
-            nmean[u, i] = work.tile([P, 1], F32, name="nmean", tag="nmean", bufs=8)
-            nc.gpsimd.tensor_scalar(
-                out=nmean[u, i][:], in0=total[u][:, i : i + 1], scalar1=-1.0 / C, scalar2=0.0, op0=ALU.mult, op1=ALU.add
-            )
+            nmean[u] = work.tile([P, len(tiles(u))], F32, name="nmean", tag="nmean")
+            nc.scalar.activation(out=nmean[u][:], in_=total[u][:], func=ACT.Copy, scale=-1.0 / C)
 
         def variance(u, i):
             if i in tiles(u):
@@ -184,17 +189,26 @@ def tile_linearattention_pb_kernel(tc, h_attn, xn, Wout_words, Wout_scales, bout
                 out=rstd[u][:], in_=sumsq[u][:], func=ACT.Abs_reciprocal_sqrt, bias=EPS, scale=1.0 / C**3
             )
 
-        def normalise(u, i):
-            if i in tiles(u):
-                z[u, i] = work.tile([P, C], F32, name="z", tag="z", bufs=4)
-                eng = nc.gpsimd
-                eng.tensor_scalar(
+        def normalise(u, i, vector):
+            if i not in tiles(u) or (u < NORM_ON_SCALAR) != vector:
+                return
+            z[u, i] = work.tile([P, C], F32, name="z", tag="z", bufs=4)
+            if vector:
+                nc.vector.tensor_scalar(
                     out=z[u, i][:],
                     in0=y[u, i][:],
-                    scalar1=nmean[u, i][:],
+                    scalar1=nmean[u][:, i : i + 1],
                     scalar2=rstd[u][:, i : i + 1],
                     op0=ALU.add,
                     op1=ALU.mult,
+                )
+            else:
+                shift = work.tile([P, 1], F32, name="shift", tag="shift")
+                nc.scalar.activation(
+                    out=shift[:], in_=nmean[u][:, i : i + 1], func=ACT.Copy, scale=rstd[u][:, i : i + 1]
+                )
+                nc.scalar.activation(
+                    out=z[u, i][:], in_=y[u, i][:], func=ACT.Identity, scale=rstd[u][:, i : i + 1], bias=shift[:]
                 )
 
         def transpose(u, i):
@@ -209,21 +223,25 @@ def tile_linearattention_pb_kernel(tc, h_attn, xn, Wout_words, Wout_scales, bout
             for j in range(CH):
                 nc.tensor.transpose(zt[u, j][:, i * TILE : (i + 1) * TILE], z[u, i][:, j * P : (j + 1) * P], ident[:])
 
-        def finish(u):
+        def finish(u, chunks):
             if not tiles(u):
                 return
-            lo, hi = UNITS[u]
-            o = keep.tile([P, CH, hi - lo], F32, name="out_%d" % u)
-            for j in range(CH):
+            first, last = [s for s in STORES if s[0] <= u <= s[1]][0]
+            lo, hi = UNITS[first][0], UNITS[last][1]
+            if first not in outs:
+                outs[first] = keep.tile([P, CH, hi - lo], F32, name="out_%d" % first)
+            o = outs[first]
+            for j in chunks:
                 nc.vector.scalar_tensor_tensor(
-                    out=o[:, j, :],
+                    out=o[:, j, UNITS[u][0] - lo : UNITS[u][1] - lo],
                     in0=zt[u, j],
                     scalar=gain4[:, j : j + 1],
                     in1=res[u][:, j, :],
                     op0=ALU.mult,
                     op1=ALU.add,
                 )
-            nc.sync.dma_start(out=out_v[lo // N, :, :, lo % N : lo % N + hi - lo], in_=o[:])
+            if u == last and CH - 1 in chunks:
+                nc.sync.dma_start(out=out_v[lo // N, :, :, lo % N : lo % N + hi - lo], in_=o[:])
 
         for g in range(PASSES):
             interleave(0, g, False)
@@ -231,24 +249,26 @@ def tile_linearattention_pb_kernel(tc, h_attn, xn, Wout_words, Wout_scales, bout
         for s in range(len(UNITS) + 3):
             variance(s - 2, 0)
             variance(s - 2, 1)
-            interleave(s + 1, 0, False)
+            negate_mean(s - 2)
             inverse_std(s - 2)
+            normalise(s - 2, 0, False)
+            normalise(s - 2, 1, False)
+            for g in range(PASSES):
+                interleave(s + 1, g, False)
             interleave(s, 0, True)
             interleave(s, 1, True)
             quantise(s, 0)
-            interleave(s, 2, True)
-            quantise(s, 1)
-            quantise(s, 2)
             multiply(s, 0)
+            interleave(s, 2, True)
             add_bias(s - 1, 0)
-            negate_mean(s - 1, 0)
-            add_bias(s - 1, 1)
-            interleave(s + 1, 1, False)
-            interleave(s + 1, 2, False)
-            finish(s - 3)
-            normalise(s - 2, 0)
-            normalise(s - 2, 1)
-            negate_mean(s - 1, 1)
-            transpose(s - 2, 0)
+            quantise(s, 1)
             multiply(s, 1)
+            add_bias(s - 1, 1)
+            finish(s - 3, (0, 1))
+            normalise(s - 2, 0, True)
+            transpose(s - 2, 0)
+            quantise(s, 2)
+            multiply(s, 2)
+            normalise(s - 2, 1, True)
             transpose(s - 2, 1)
+            finish(s - 3, (2, 3))

@@ -32,8 +32,8 @@ NORM_ON_SCALAR = 7
 def tile_linearattention_pb_kernel(tc, h_attn, xn, Wout_words, Wout_scales, bout, outnorm_g, out):
     nc = tc.nc
     h_v = h_attn.rearrange("b (g p j) y x -> b g p j (y x)", p=P, j=PACK)
-    xn_v = xn.rearrange("b (p j) y x -> b p j (y x)", j=CH)
-    out_v = out.rearrange("b (p j) y x -> b p j (y x)", j=CH)
+    xn_v = xn.rearrange("b (j p) y x -> b p j (y x)", p=P)
+    out_v = out.rearrange("b (j p) y x -> b p j (y x)", p=P)
 
     with ExitStack() as ctx:
         keep = ctx.enter_context(tc.tile_pool(name="keep", bufs=1))
@@ -63,9 +63,12 @@ def tile_linearattention_pb_kernel(tc, h_attn, xn, Wout_words, Wout_scales, bout
 
         words = keep.tile([P, PASSES, 2 * C], U8, name="words", align_bytes=64)
         w_scale = keep.tile([P, PASSES, C], U8, name="w_scale", align_bytes=64)
-        bias4 = keep.tile([P, CH], BF16, name="bias4")
-        gain4 = keep.tile([P, CH], BF16, name="gain4")
-        nc.gpsimd.dma_start(out=bias4[:], in_=bout.rearrange("(p j) -> p j", j=CH))
+        row = keep.tile([P, 2 * C], BF16, name="row")
+        nc.vector.memset(row[:], 0.0)
+        ident = keep.tile([P, P], F32, name="ident")
+        make_identity(nc, ident[:])
+        nc.gpsimd.dma_start(out=row[0:1, 0:C], in_=bout.rearrange("(o c) -> o c", o=1))
+        nc.gpsimd.dma_start(out=row[0:1, C : 2 * C], in_=outnorm_g.rearrange("o c y x -> o (c y x)"))
         for q in range(4):
             nc.scalar.dma_start(
                 out=w_scale[32 * q : 32 * q + 4, :, :].bitcast(I32),
@@ -82,15 +85,17 @@ def tile_linearattention_pb_kernel(tc, h_attn, xn, Wout_words, Wout_scales, bout
         load_xn(1)
         load_xn(2)
 
-        ident = keep.tile([P, P], F32, name="ident")
-        make_identity(nc, ident[:])
-        nc.gpsimd.dma_start(out=gain4[:], in_=outnorm_g.rearrange("o (p j) y x -> p (o j y x)", j=CH))
-        bias4f = keep.tile([P, CH], F32, name="bias4f")
-        nc.scalar.activation(out=bias4f[:], in_=bias4[:], func=ACT.Copy)
+        ones = keep.tile([P, P], BF16, name="ones")
+        nc.scalar.activation(out=ones[:], in_=ident[:], func=ACT.Abs_reciprocal_sqrt, bias=1.0, scale=0.0)
         bias_ps = tr_pool.tile([P, C], F32, name="bias_ps", tag="tr")
+        nc.tensor.matmul(bias_ps[:], lhsT=ones[:], rhs=row[:, 0:C], start=True, stop=True)
+        gain_ps = tr_pool.tile([P, CH], F32, name="gain_ps", tag="tr")
         for j in range(CH):
-            nc.tensor.transpose(bias_ps[:, j * P : (j + 1) * P], bias4f[:, j : j + 1].to_broadcast([P, P]), ident[:])
+            nc.tensor.matmul(
+                gain_ps[:, j : j + 1], lhsT=row[:, C + j * P : C + (j + 1) * P], rhs=ones[:, 0:1], start=True, stop=True
+            )
         bias_all = keep.tile([P, C], F32, name="bias_all")
+        gain4 = keep.tile([P, CH], F32, name="gain4")
 
         grouped, codes, scales, acc, y, z, total, sumsq, rstd, nmean, zt = ({} for k in range(11))
 
@@ -99,7 +104,7 @@ def tile_linearattention_pb_kernel(tc, h_attn, xn, Wout_words, Wout_scales, bout
 
         def vector_columns(u, g):
             width = UNITS[u][1] - UNITS[u][0]
-            return width if (u == 0 and g != 1) or (0 < u < 3 and g > 0) else (width * 5 // 8 if g == 2 and u < 7 else 0)
+            return width if (u == 0 and g != 1) or (0 < u < 3 and g > 0) else (width * 4 // 8 if g == 2 and u < 7 else 0)
 
         def interleave(u, g, vector):
             if not tiles(u):
@@ -152,10 +157,10 @@ def tile_linearattention_pb_kernel(tc, h_attn, xn, Wout_words, Wout_scales, bout
                     total[u] = work.tile([P, len(tiles(u))], F32, name="total", tag="total")
                 y[u, i] = work.tile([P, C], F32, name="y", tag="y", bufs=6)
                 nc.vector.scalar_tensor_tensor(
-                    out=y[u, i][:].rearrange("n (j p) -> n j p", j=CH),
-                    in0=acc[u, i][:].rearrange("n (p j) -> n j p", j=CH),
+                    out=y[u, i][:],
+                    in0=acc[u, i][:],
                     scalar=1.0,
-                    in1=bias_all[:].rearrange("n (j p) -> n j p", j=CH),
+                    in1=bias_all[:],
                     op0=ALU.mult,
                     op1=ALU.add,
                     accum_out=total[u][:, i : i + 1],
@@ -246,6 +251,7 @@ def tile_linearattention_pb_kernel(tc, h_attn, xn, Wout_words, Wout_scales, bout
         for g in range(PASSES):
             interleave(0, g, False)
         nc.scalar.copy(out=bias_all[:], in_=bias_ps[:])
+        nc.scalar.copy(out=gain4[:], in_=gain_ps[:])
         for s in range(len(UNITS) + 3):
             variance(s - 2, 0)
             variance(s - 2, 1)
@@ -260,15 +266,22 @@ def tile_linearattention_pb_kernel(tc, h_attn, xn, Wout_words, Wout_scales, bout
             quantise(s, 0)
             multiply(s, 0)
             interleave(s, 2, True)
+            late = [g for g in (1, 2) if s < 7]
+            for g in (1, 2):
+                if g not in late:
+                    quantise(s, g)
+                    multiply(s, g)
             add_bias(s - 1, 0)
-            quantise(s, 1)
-            multiply(s, 1)
+            if late:
+                quantise(s, 1)
+                multiply(s, 1)
             add_bias(s - 1, 1)
             finish(s - 3, (0, 1))
             normalise(s - 2, 0, True)
             transpose(s - 2, 0)
-            quantise(s, 2)
-            multiply(s, 2)
+            if late:
+                quantise(s, 2)
+                multiply(s, 2)
             normalise(s - 2, 1, True)
             transpose(s - 2, 1)
             finish(s - 3, (2, 3))

@@ -21,19 +21,21 @@ P = 128
 PACK = 4
 PASSES = E // (P * PACK)
 TILE = 128
-CH = C // P
-H_RANGES = [(0, 256), (256, 512), (512, 1024), (1024, 2048)]
+CHUNKS = C // P
+
+WIDE_UNITS = 7
+UNITS = [(256 * u, 256 * (u + 1)) for u in range(WIDE_UNITS)] + [(1792, 1920), (1920, 2048)]
+H_RANGES = [(0, 256), (256, 512), (512, 1024), (1024, 1536), (1536, 2048)]
 XN_RANGES = [(0, 512), (512, 1024), (1024, 2048)]
-UNITS = [(0, 256), (256, 512), (512, 768), (768, 1024), (1024, 1280), (1280, 1536), (1536, 1792), (1792, 1920), (1920, 2048)]
-STORES = [(0, 1), (2, 3), (4, 4), (5, 5), (6, 6), (7, 7), (8, 8)]
-NORM_ON_SCALAR = 7
+PAIRED_UNITS = 4
+HEAD_UNITS = 3
 
 
 def tile_linearattention_pb_kernel(tc, h_attn, xn, Wout_words, Wout_scales, bout, outnorm_g, out):
     nc = tc.nc
-    h_v = h_attn.rearrange("b (g p j) y x -> b g p j (y x)", p=P, j=PACK)
-    xn_v = xn.rearrange("b (j p) y x -> b p j (y x)", p=P)
-    out_v = out.rearrange("b (j p) y x -> b p j (y x)", p=P)
+    h_view = h_attn.rearrange("b (g p t) y x -> b g p t (y x)", p=P, t=PACK)
+    xn_view = xn.rearrange("b (j p) y x -> b p j (y x)", p=P)
+    out_view = out.rearrange("b (j p) y x -> b p j (y x)", p=P)
 
     with ExitStack() as ctx:
         keep = ctx.enter_context(tc.tile_pool(name="keep", bufs=1))
@@ -42,101 +44,103 @@ def tile_linearattention_pb_kernel(tc, h_attn, xn, Wout_words, Wout_scales, bout
         tr_pool = ctx.enter_context(tc.psum_pool(name="tr", bufs=4))
         ctx.enter_context(tc.manual_schedule())
 
-        raw, res, outs = {}, {}, {}
+        raw, residual, staged = {}, {}, {}
 
-        def load_h(r, passes=range(PASSES)):
+        def load_h(r, passes):
             lo, hi = H_RANGES[r]
             for g in passes:
-                t = keep.tile([P, PACK, hi - lo], BF16, name="raw_%d_%d" % (r, g))
-                nc.sync.dma_start(out=t[:], in_=h_v[lo // N, g, :, :, lo % N : lo % N + hi - lo])
-                for u, (a, b) in enumerate(UNITS):
-                    if lo <= a < hi:
-                        raw[u, g] = t[:, :, a - lo : b - lo]
+                rows = keep.tile([P, PACK, hi - lo], BF16, name="raw_%d_%d" % (r, g))
+                nc.sync.dma_start(out=rows[:], in_=h_view[lo // N, g, :, :, lo % N : lo % N + hi - lo])
+                for u, (first, last) in enumerate(UNITS):
+                    if lo <= first < hi:
+                        raw[u, g] = rows[:, :, first - lo : last - lo]
 
         def load_xn(r):
             lo, hi = XN_RANGES[r]
-            t = keep.tile([P, CH, hi - lo], BF16, name="xn_%d" % r)
-            nc.sync.dma_start(out=t[:], in_=xn_v[lo // N, :, :, lo % N : lo % N + hi - lo])
-            for u, (a, b) in enumerate(UNITS):
-                if lo <= a < hi:
-                    res[u] = t[:, :, a - lo : b - lo]
+            rows = keep.tile([P, CHUNKS, hi - lo], BF16, name="xn_%d" % r)
+            nc.sync.dma_start(out=rows[:], in_=xn_view[lo // N, :, :, lo % N : lo % N + hi - lo])
+            for u, (first, last) in enumerate(UNITS):
+                if lo <= first < hi:
+                    residual[u] = rows[:, :, first - lo : last - lo]
 
         words = keep.tile([P, PASSES, 2 * C], U8, name="words", align_bytes=64)
         w_scale = keep.tile([P, PASSES, C], U8, name="w_scale", align_bytes=64)
-        row = keep.tile([P, 2 * C], BF16, name="row")
-        nc.vector.memset(row[:], 0.0)
+        bias_gain = keep.tile([P, 2 * C], BF16, name="bias_gain")
+        nc.vector.memset(bias_gain[:], 0.0)
         ident = keep.tile([P, P], F32, name="ident")
         make_identity(nc, ident[:])
-        nc.gpsimd.dma_start(out=row[0:1, 0:C], in_=bout.rearrange("(o c) -> o c", o=1))
-        nc.gpsimd.dma_start(out=row[0:1, C : 2 * C], in_=outnorm_g.rearrange("o c y x -> o (c y x)"))
         for q in range(4):
             nc.scalar.dma_start(
                 out=w_scale[32 * q : 32 * q + 4, :, :].bitcast(I32),
                 in_=Wout_scales[:, 4 * q : 4 * q + 4, :].rearrange("g r n -> r g n").bitcast(I32),
             )
 
-        load_h(0)
+        load_h(0, range(PASSES))
         nc.sync.dma_start(out=words[:].bitcast(I32), in_=Wout_words.rearrange("g p n -> p g n").bitcast(I32))
-        load_h(1)
-        load_h(2)
-        load_h(3, [0])
-        load_xn(0)
-        load_h(3, [1, 2])
-        load_xn(1)
-        load_xn(2)
-
         ones = keep.tile([P, P], BF16, name="ones")
         nc.scalar.activation(out=ones[:], in_=ident[:], func=ACT.Abs_reciprocal_sqrt, bias=1.0, scale=0.0)
-        bias_ps = tr_pool.tile([P, C], F32, name="bias_ps", tag="tr")
-        nc.tensor.matmul(bias_ps[:], lhsT=ones[:], rhs=row[:, 0:C], start=True, stop=True)
-        gain_ps = tr_pool.tile([P, CH], F32, name="gain_ps", tag="tr")
-        for j in range(CH):
-            nc.tensor.matmul(
-                gain_ps[:, j : j + 1], lhsT=row[:, C + j * P : C + (j + 1) * P], rhs=ones[:, 0:1], start=True, stop=True
-            )
-        bias_all = keep.tile([P, C], F32, name="bias_all")
-        gain4 = keep.tile([P, CH], F32, name="gain4")
+        nc.sync.dma_start(out=bias_gain[0:1, 0:C], in_=bout.rearrange("(o c) -> o c", o=1))
+        nc.sync.dma_start(out=bias_gain[0:1, C : 2 * C], in_=outnorm_g.rearrange("o c y x -> o (c y x)"))
+        load_h(1, range(PASSES))
+        load_h(2, range(PASSES))
+        load_xn(0)
+        load_h(3, range(PASSES))
+        load_xn(1)
+        load_h(4, range(PASSES))
+        load_xn(2)
 
-        grouped, codes, scales, acc, y, z, total, sumsq, rstd, nmean, zt = ({} for k in range(11))
+        bias_ps = tr_pool.tile([P, C], F32, name="bias_ps", tag="tr")
+        nc.tensor.matmul(bias_ps[:], lhsT=ones[:], rhs=bias_gain[:, 0:C], start=True, stop=True)
+        gain_ps = tr_pool.tile([P, CHUNKS], F32, name="gain_ps", tag="tr")
+        for j in range(CHUNKS):
+            nc.tensor.matmul(
+                gain_ps[:, j : j + 1],
+                lhsT=bias_gain[:, C + j * P : C + (j + 1) * P],
+                rhs=ones[:, 0:1],
+                start=True,
+                stop=True,
+            )
+        bias = keep.tile([P, C], F32, name="bias")
+        gain = keep.tile([P, CHUNKS], F32, name="gain")
+
+        grouped, codes, scales, acc, y, z, total, sumsq, rstd, neg_mean, z_t = ({} for k in range(11))
 
         def tiles(u):
-            return range((UNITS[u][1] - UNITS[u][0]) // TILE) if 0 <= u < len(UNITS) else range(0)
+            return range((UNITS[u][1] - UNITS[u][0]) // TILE) if u >= 0 else range(0)
 
         def vector_columns(u, g):
             width = UNITS[u][1] - UNITS[u][0]
-            return width if (u == 0 and g != 1) or (0 < u < 3 and g > 0) else (width * 4 // 8 if g == 2 and u < 7 else 0)
+            if u < HEAD_UNITS:
+                scalar_pass = 1 if u == 0 else 0
+                return 0 if g == scalar_pass else width
+            return width // 2 if u < WIDE_UNITS and g == PASSES - 1 else 0
 
-        def interleave(u, g, vector):
-            if not tiles(u):
-                return
+        def interleave(u, g, on_vector):
             width = UNITS[u][1] - UNITS[u][0]
             cut = width - vector_columns(u, g)
-            cols = slice(cut, width) if vector else slice(0, cut)
+            cols = slice(cut, width) if on_vector else slice(0, cut)
             if cols.start == cols.stop:
                 return
             if (u, g) not in grouped:
                 grouped[u, g] = work.tile(
                     [P, width, PACK], BF16, name="grouped", tag="grouped", bufs=7, align_bytes=64
                 )
-            dst = grouped[u, g][:, cols, :].rearrange("p (c i) t -> p c t i", i=4)
-            src = raw[u, g][:, :, cols].rearrange("p t (c i) -> p c t i", i=4)
-            if vector:
+            dst = grouped[u, g][:, cols, :]
+            src = raw[u, g][:, :, cols].rearrange("p t n -> p n t")
+            if on_vector:
                 nc.vector.tensor_copy(out=dst, in_=src)
             else:
                 nc.scalar.copy(out=dst, in_=src)
 
-        def quantise(u, g):
-            if not tiles(u):
-                return
-            width = len(tiles(u)) * TILE
-            cd = work.tile([P, width], U32, name="codes", tag="codes", bufs=9, align_bytes=64)
-            sc = work.tile([P, width], U8, name="scales", tag="scales", bufs=9, align_bytes=64)
-            codes[u, g], scales[u, g] = cd, sc
+        def quantise_and_multiply(u, g):
+            width = UNITS[u][1] - UNITS[u][0]
+            codes[u, g] = work.tile([P, width], U32, name="codes", tag="codes", bufs=9, align_bytes=64)
+            scales[u, g] = work.tile([P, width], U8, name="scales", tag="scales", bufs=9, align_bytes=64)
             nc.vector.quantize_mx(
-                out=cd[:].bitcast(E5M2X4), scales=sc[:], in_=grouped[u, g][:].rearrange("p n t -> p (n t)")
+                out=codes[u, g][:].bitcast(E5M2X4),
+                scales=scales[u, g][:],
+                in_=grouped[u, g][:].rearrange("p n t -> p (n t)"),
             )
-
-        def multiply(u, g):
             for i in tiles(u):
                 if g == 0:
                     acc[u, i] = acc_pool.tile([P, C], F32, name="acc", tag="acc")
@@ -152,30 +156,26 @@ def tile_linearattention_pb_kernel(tc, h_attn, xn, Wout_words, Wout_scales, bout
                 )
 
         def add_bias(u, i):
-            if i in tiles(u):
-                if i == 0:
-                    total[u] = work.tile([P, len(tiles(u))], F32, name="total", tag="total")
-                y[u, i] = work.tile([P, C], F32, name="y", tag="y", bufs=6)
-                nc.vector.scalar_tensor_tensor(
-                    out=y[u, i][:],
-                    in0=acc[u, i][:],
-                    scalar=1.0,
-                    in1=bias_all[:],
-                    op0=ALU.mult,
-                    op1=ALU.add,
-                    accum_out=total[u][:, i : i + 1],
-                )
+            if i not in tiles(u):
+                return
+            if i == 0:
+                total[u] = work.tile([P, len(tiles(u))], F32, name="total", tag="total")
+            y[u, i] = work.tile([P, C], F32, name="y", tag="y", bufs=6)
+            nc.vector.scalar_tensor_tensor(
+                out=y[u, i][:],
+                in0=acc[u, i][:],
+                scalar=1.0,
+                in1=bias[:],
+                op0=ALU.mult,
+                op1=ALU.add,
+                accum_out=total[u][:, i : i + 1],
+            )
 
-        def negate_mean(u):
+        def statistics(u):
             if not tiles(u):
                 return
-            nmean[u] = work.tile([P, len(tiles(u))], F32, name="nmean", tag="nmean")
-            nc.scalar.activation(out=nmean[u][:], in_=total[u][:], func=ACT.Copy, scale=-1.0 / C)
-
-        def variance(u, i):
-            if i in tiles(u):
-                if i == 0:
-                    sumsq[u] = work.tile([P, len(tiles(u))], F32, name="sumsq", tag="sumsq")
+            sumsq[u] = work.tile([P, len(tiles(u))], F32, name="sumsq", tag="sumsq")
+            for i in tiles(u):
                 squares = work.tile([P, C], BF16, name="squares", tag="squares", bufs=2)
                 nc.scalar.activation(
                     out=squares[:],
@@ -185,103 +185,118 @@ def tile_linearattention_pb_kernel(tc, h_attn, xn, Wout_words, Wout_scales, bout
                     scale=-float(C),
                     accum_out=sumsq[u][:, i : i + 1],
                 )
-
-        def inverse_std(u):
-            if not tiles(u):
-                return
+            neg_mean[u] = work.tile([P, len(tiles(u))], F32, name="neg_mean", tag="neg_mean")
+            nc.scalar.activation(out=neg_mean[u][:], in_=total[u][:], func=ACT.Copy, scale=-1.0 / C)
             rstd[u] = work.tile([P, len(tiles(u))], F32, name="rstd", tag="rstd")
             nc.scalar.activation(
                 out=rstd[u][:], in_=sumsq[u][:], func=ACT.Abs_reciprocal_sqrt, bias=EPS, scale=1.0 / C**3
             )
 
-        def normalise(u, i, vector):
-            if i not in tiles(u) or (u < NORM_ON_SCALAR) != vector:
-                return
-            z[u, i] = work.tile([P, C], F32, name="z", tag="z", bufs=4)
-            if vector:
-                nc.vector.tensor_scalar(
-                    out=z[u, i][:],
-                    in0=y[u, i][:],
-                    scalar1=nmean[u][:, i : i + 1],
-                    scalar2=rstd[u][:, i : i + 1],
-                    op0=ALU.add,
-                    op1=ALU.mult,
-                )
-            else:
-                shift = work.tile([P, 1], F32, name="shift", tag="shift")
-                nc.scalar.activation(
-                    out=shift[:], in_=nmean[u][:, i : i + 1], func=ACT.Copy, scale=rstd[u][:, i : i + 1]
-                )
-                nc.scalar.activation(
-                    out=z[u, i][:], in_=y[u, i][:], func=ACT.Identity, scale=rstd[u][:, i : i + 1], bias=shift[:]
-                )
-
-        def transpose(u, i):
+        def normalise_on_vector(u, i):
             if i not in tiles(u):
                 return
-            n = len(tiles(u))
-            if i == 0:
-                for k in range(n):
-                    bank = tr_pool.tile([P, C], F32, name="zt", tag="tr")
-                    for j in range(CH // n):
-                        zt[u, k * (CH // n) + j] = bank[:, j * n * TILE : (j + 1) * n * TILE]
-            for j in range(CH):
-                nc.tensor.transpose(zt[u, j][:, i * TILE : (i + 1) * TILE], z[u, i][:, j * P : (j + 1) * P], ident[:])
+            z[u, i] = work.tile([P, C], F32, name="z", tag="z")
+            nc.vector.tensor_scalar(
+                out=z[u, i][:],
+                in0=y[u, i][:],
+                scalar1=neg_mean[u][:, i : i + 1],
+                scalar2=rstd[u][:, i : i + 1],
+                op0=ALU.add,
+                op1=ALU.mult,
+            )
 
-        def finish(u, chunks):
+        def normalise_on_scalar(u):
+            z[u, 0] = work.tile([P, C], F32, name="z", tag="z")
+            shift = work.tile([P, 1], F32, name="shift", tag="shift")
+            nc.scalar.activation(out=shift[:], in_=neg_mean[u][:], func=ACT.Copy, scale=rstd[u][:])
+            nc.scalar.activation(out=z[u, 0][:], in_=y[u, 0][:], func=ACT.Identity, scale=rstd[u][:], bias=shift[:])
+
+        def transpose(u):
+            count = len(tiles(u))
+            for k in range(count):
+                bank = tr_pool.tile([P, C], F32, name="z_t", tag="tr")
+                for j in range(CHUNKS // count):
+                    z_t[u, k * (CHUNKS // count) + j] = bank[:, j * count * TILE : (j + 1) * count * TILE]
+            for i in tiles(u):
+                for j in range(CHUNKS):
+                    nc.tensor.transpose(
+                        z_t[u, j][:, i * TILE : (i + 1) * TILE], z[u, i][:, j * P : (j + 1) * P], ident[:]
+                    )
+
+        def finish(u, half):
             if not tiles(u):
                 return
-            first, last = [s for s in STORES if s[0] <= u <= s[1]][0]
+            first, last = (u - u % 2, u - u % 2 + 1) if u < PAIRED_UNITS else (u, u)
             lo, hi = UNITS[first][0], UNITS[last][1]
-            if first not in outs:
-                outs[first] = keep.tile([P, CH, hi - lo], F32, name="out_%d" % first)
-            o = outs[first]
-            for j in chunks:
+            if first not in staged:
+                staged[first] = keep.tile([P, CHUNKS, hi - lo], F32, name="staged_%d" % first)
+            chunks = slice(2 * half, 2 * half + 2)
+            for j in range(chunks.start, chunks.stop):
                 nc.vector.scalar_tensor_tensor(
-                    out=o[:, j, UNITS[u][0] - lo : UNITS[u][1] - lo],
-                    in0=zt[u, j],
-                    scalar=gain4[:, j : j + 1],
-                    in1=res[u][:, j, :],
+                    out=staged[first][:, j, UNITS[u][0] - lo : UNITS[u][1] - lo],
+                    in0=z_t[u, j],
+                    scalar=gain[:, j : j + 1],
+                    in1=residual[u][:, j, :],
                     op0=ALU.mult,
                     op1=ALU.add,
                 )
-            if u == last and CH - 1 in chunks:
-                nc.sync.dma_start(out=out_v[lo // N, :, :, lo % N : lo % N + hi - lo], in_=o[:])
+            if u == last:
+                nc.sync.dma_start(
+                    out=out_view[lo // N, :, chunks, lo % N : lo % N + hi - lo], in_=staged[first][:, chunks, :]
+                )
 
         for g in range(PASSES):
             interleave(0, g, False)
-        nc.scalar.copy(out=bias_all[:], in_=bias_ps[:])
-        nc.scalar.copy(out=gain4[:], in_=gain_ps[:])
-        for s in range(len(UNITS) + 3):
-            variance(s - 2, 0)
-            variance(s - 2, 1)
-            negate_mean(s - 2)
-            inverse_std(s - 2)
-            normalise(s - 2, 0, False)
-            normalise(s - 2, 1, False)
+        for s in range(WIDE_UNITS):
+            statistics(s - 2)
             for g in range(PASSES):
                 interleave(s + 1, g, False)
             interleave(s, 0, True)
             interleave(s, 1, True)
-            quantise(s, 0)
-            multiply(s, 0)
+            quantise_and_multiply(s, 0)
             interleave(s, 2, True)
-            late = [g for g in (1, 2) if s < 7]
-            for g in (1, 2):
-                if g not in late:
-                    quantise(s, g)
-                    multiply(s, g)
             add_bias(s - 1, 0)
-            if late:
-                quantise(s, 1)
-                multiply(s, 1)
+            quantise_and_multiply(s, 1)
             add_bias(s - 1, 1)
-            finish(s - 3, (0, 1))
-            normalise(s - 2, 0, True)
-            transpose(s - 2, 0)
-            if late:
-                quantise(s, 2)
-                multiply(s, 2)
-            normalise(s - 2, 1, True)
-            transpose(s - 2, 1)
-            finish(s - 3, (2, 3))
+            finish(s - 3, 0)
+            normalise_on_vector(s - 2, 0)
+            quantise_and_multiply(s, 2)
+            normalise_on_vector(s - 2, 1)
+            transpose(s - 2)
+            finish(s - 3, 1)
+            if s == 0:
+                nc.scalar.copy(out=bias[:], in_=bias_ps[:])
+                nc.scalar.copy(out=gain[:], in_=gain_ps[:])
+
+        a, b = WIDE_UNITS, WIDE_UNITS + 1
+        statistics(a - 2)
+        for g in range(PASSES):
+            interleave(b, g, False)
+        for g in range(PASSES):
+            quantise_and_multiply(a, g)
+        add_bias(a - 1, 0)
+        add_bias(a - 1, 1)
+        finish(a - 3, 0)
+        normalise_on_vector(a - 2, 0)
+        normalise_on_vector(a - 2, 1)
+        transpose(a - 2)
+        finish(a - 3, 1)
+        statistics(a - 1)
+        for g in range(PASSES):
+            quantise_and_multiply(b, g)
+        add_bias(a, 0)
+        finish(a - 2, 0)
+        add_bias(b, 0)
+        normalise_on_vector(a - 1, 0)
+        normalise_on_vector(a - 1, 1)
+        transpose(a - 1)
+        finish(a - 2, 1)
+        for u in (a, b):
+            statistics(u)
+            normalise_on_scalar(u)
+        finish(a - 1, 0)
+        finish(a - 1, 1)
+        for u in (a, b):
+            transpose(u)
+            finish(u, 0)
+            finish(u, 1)

from contextlib import ExitStack

import concourse.mybir as mybir
from concourse.masks import make_identity

B, C, E, N = 2, 512, 1536, 1024
EPS = 1e-5
FLOPS = 2 * B * C * E * N

F32 = mybir.dt.float32
BF16 = mybir.dt.bfloat16
U32 = mybir.dt.uint32
I32 = mybir.dt.int32
U8 = mybir.dt.uint8
E5M2X4 = mybir.dt.float8_e5m2_x4
E2M1X4 = mybir.dt.float4_e2m1fn_x4
ALU = mybir.AluOpType
ACT = mybir.ActivationFunctionType

P = 128
PACK = 4
PASSES = E // (P * PACK)
TILE = 128
CHUNKS = C // P

WIDE_UNITS = 7
UNITS = [(256 * u, 256 * (u + 1)) for u in range(WIDE_UNITS)] + [(1792, 1920), (1920, 2048)]
H_RANGES = [(0, 256), (256, 512), (512, 1024), (1024, 1536), (1536, 2048)]
XN_RANGES = [(0, 512), (512, 1024), (1024, 2048)]
PAIRED_UNITS = 4
HEAD_UNITS = 3


def tile_linearattention_pb_kernel(tc, h_attn, xn, Wout_words, Wout_scales, bout, outnorm_g, out):
    nc = tc.nc
    h_view = h_attn.rearrange("b (g p t) y x -> b g p t (y x)", p=P, t=PACK)
    xn_view = xn.rearrange("b (j p) y x -> b p j (y x)", p=P)
    out_view = out.rearrange("b (j p) y x -> b p j (y x)", p=P)

    with ExitStack() as ctx:
        keep = ctx.enter_context(tc.tile_pool(name="keep", bufs=1))
        work = ctx.enter_context(tc.tile_pool(name="work", bufs=4))
        acc_pool = ctx.enter_context(tc.psum_pool(name="acc", bufs=4))
        tr_pool = ctx.enter_context(tc.psum_pool(name="tr", bufs=4))
        ctx.enter_context(tc.manual_schedule())

        raw, residual, staged = {}, {}, {}

        def load_h(r, passes):
            lo, hi = H_RANGES[r]
            for g in passes:
                rows = keep.tile([P, PACK, hi - lo], BF16, name="raw_%d_%d" % (r, g))
                nc.sync.dma_start(out=rows[:], in_=h_view[lo // N, g, :, :, lo % N : lo % N + hi - lo])
                for u, (first, last) in enumerate(UNITS):
                    if lo <= first < hi:
                        raw[u, g] = rows[:, :, first - lo : last - lo]

        def load_xn(r):
            lo, hi = XN_RANGES[r]
            rows = keep.tile([P, CHUNKS, hi - lo], BF16, name="xn_%d" % r)
            nc.sync.dma_start(out=rows[:], in_=xn_view[lo // N, :, :, lo % N : lo % N + hi - lo])
            for u, (first, last) in enumerate(UNITS):
                if lo <= first < hi:
                    residual[u] = rows[:, :, first - lo : last - lo]

        words = keep.tile([P, PASSES, 2 * C], U8, name="words", align_bytes=64)
        w_scale = keep.tile([P, PASSES, C], U8, name="w_scale", align_bytes=64)
        bias_gain = keep.tile([P, 2 * C], BF16, name="bias_gain")
        nc.vector.memset(bias_gain[:], 0.0)
        ident = keep.tile([P, P], F32, name="ident")
        make_identity(nc, ident[:])
        for q in range(4):
            nc.scalar.dma_start(
                out=w_scale[32 * q : 32 * q + 4, :, :].bitcast(I32),
                in_=Wout_scales[:, 4 * q : 4 * q + 4, :].rearrange("g r n -> r g n").bitcast(I32),
            )

        load_h(0, range(PASSES))
        nc.sync.dma_start(out=words[:].bitcast(I32), in_=Wout_words.rearrange("g p n -> p g n").bitcast(I32))
        ones = keep.tile([P, P], BF16, name="ones")
        nc.scalar.activation(out=ones[:], in_=ident[:], func=ACT.Abs_reciprocal_sqrt, bias=1.0, scale=0.0)
        nc.sync.dma_start(out=bias_gain[0:1, 0:C], in_=bout.rearrange("(o c) -> o c", o=1))
        nc.sync.dma_start(out=bias_gain[0:1, C : 2 * C], in_=outnorm_g.rearrange("o c y x -> o (c y x)"))
        load_h(1, range(PASSES))
        load_h(2, range(PASSES))
        load_xn(0)
        load_h(3, range(PASSES))
        load_xn(1)
        load_h(4, range(PASSES))
        load_xn(2)

        bias_ps = tr_pool.tile([P, C], F32, name="bias_ps", tag="tr")
        nc.tensor.matmul(bias_ps[:], lhsT=ones[:], rhs=bias_gain[:, 0:C], start=True, stop=True)
        gain_ps = tr_pool.tile([P, CHUNKS], F32, name="gain_ps", tag="tr")
        for j in range(CHUNKS):
            nc.tensor.matmul(
                gain_ps[:, j : j + 1],
                lhsT=bias_gain[:, C + j * P : C + (j + 1) * P],
                rhs=ones[:, 0:1],
                start=True,
                stop=True,
            )
        bias = keep.tile([P, C], F32, name="bias")
        gain = keep.tile([P, CHUNKS], F32, name="gain")

        grouped, codes, scales, acc, y, z, total, sumsq, rstd, neg_mean, z_t = ({} for k in range(11))

        def tiles(u):
            return range((UNITS[u][1] - UNITS[u][0]) // TILE) if u >= 0 else range(0)

        def vector_columns(u, g):
            width = UNITS[u][1] - UNITS[u][0]
            if u < HEAD_UNITS:
                scalar_pass = 1 if u == 0 else 0
                return 0 if g == scalar_pass else width
            return width // 2 if u < WIDE_UNITS and g == PASSES - 1 else 0

        def interleave(u, g, on_vector):
            width = UNITS[u][1] - UNITS[u][0]
            cut = width - vector_columns(u, g)
            cols = slice(cut, width) if on_vector else slice(0, cut)
            if cols.start == cols.stop:
                return
            if (u, g) not in grouped:
                grouped[u, g] = work.tile(
                    [P, width, PACK], BF16, name="grouped", tag="grouped", bufs=7, align_bytes=64
                )
            dst = grouped[u, g][:, cols, :]
            src = raw[u, g][:, :, cols].rearrange("p t n -> p n t")
            if on_vector:
                nc.vector.tensor_copy(out=dst, in_=src)
            else:
                nc.scalar.copy(out=dst, in_=src)

        def quantise_and_multiply(u, g):
            width = UNITS[u][1] - UNITS[u][0]
            codes[u, g] = work.tile([P, width], U32, name="codes", tag="codes", bufs=9, align_bytes=64)
            scales[u, g] = work.tile([P, width], U8, name="scales", tag="scales", bufs=9, align_bytes=64)
            nc.vector.quantize_mx(
                out=codes[u, g][:].bitcast(E5M2X4),
                scales=scales[u, g][:],
                in_=grouped[u, g][:].rearrange("p n t -> p (n t)"),
            )
            for i in tiles(u):
                if g == 0:
                    acc[u, i] = acc_pool.tile([P, C], F32, name="acc", tag="acc")
                cols = slice(i * TILE, (i + 1) * TILE)
                nc.tensor.matmul_mx(
                    out=acc[u, i][:],
                    lhsT=codes[u, g][:, cols].bitcast(E5M2X4),
                    lhsT_scale=scales[u, g][:, cols],
                    rhs=words[:, g, :].bitcast(E2M1X4),
                    rhs_scale=w_scale[:, g, :],
                    start=(g == 0),
                    stop=(g == PASSES - 1),
                )

        def add_bias(u, i):
            if i not in tiles(u):
                return
            if i == 0:
                total[u] = work.tile([P, len(tiles(u))], F32, name="total", tag="total")
            y[u, i] = work.tile([P, C], F32, name="y", tag="y", bufs=6)
            nc.vector.scalar_tensor_tensor(
                out=y[u, i][:],
                in0=acc[u, i][:],
                scalar=1.0,
                in1=bias[:],
                op0=ALU.mult,
                op1=ALU.add,
                accum_out=total[u][:, i : i + 1],
            )

        def statistics(u):
            if not tiles(u):
                return
            sumsq[u] = work.tile([P, len(tiles(u))], F32, name="sumsq", tag="sumsq")
            for i in tiles(u):
                squares = work.tile([P, C], BF16, name="squares", tag="squares", bufs=2)
                nc.scalar.activation(
                    out=squares[:],
                    in_=y[u, i][:],
                    func=ACT.Square,
                    bias=total[u][:, i : i + 1],
                    scale=-float(C),
                    accum_out=sumsq[u][:, i : i + 1],
                )
            neg_mean[u] = work.tile([P, len(tiles(u))], F32, name="neg_mean", tag="neg_mean")
            nc.scalar.activation(out=neg_mean[u][:], in_=total[u][:], func=ACT.Copy, scale=-1.0 / C)
            rstd[u] = work.tile([P, len(tiles(u))], F32, name="rstd", tag="rstd")
            nc.scalar.activation(
                out=rstd[u][:], in_=sumsq[u][:], func=ACT.Abs_reciprocal_sqrt, bias=EPS, scale=1.0 / C**3
            )

        def normalise_on_vector(u, i):
            if i not in tiles(u):
                return
            z[u, i] = work.tile([P, C], F32, name="z", tag="z")
            nc.vector.tensor_scalar(
                out=z[u, i][:],
                in0=y[u, i][:],
                scalar1=neg_mean[u][:, i : i + 1],
                scalar2=rstd[u][:, i : i + 1],
                op0=ALU.add,
                op1=ALU.mult,
            )

        def normalise_on_scalar(u):
            z[u, 0] = work.tile([P, C], F32, name="z", tag="z")
            shift = work.tile([P, 1], F32, name="shift", tag="shift")
            nc.scalar.activation(out=shift[:], in_=neg_mean[u][:], func=ACT.Copy, scale=rstd[u][:])
            nc.scalar.activation(out=z[u, 0][:], in_=y[u, 0][:], func=ACT.Identity, scale=rstd[u][:], bias=shift[:])

        def transpose(u):
            count = len(tiles(u))
            for k in range(count):
                bank = tr_pool.tile([P, C], F32, name="z_t", tag="tr")
                for j in range(CHUNKS // count):
                    z_t[u, k * (CHUNKS // count) + j] = bank[:, j * count * TILE : (j + 1) * count * TILE]
            for i in tiles(u):
                for j in range(CHUNKS):
                    nc.tensor.transpose(
                        z_t[u, j][:, i * TILE : (i + 1) * TILE], z[u, i][:, j * P : (j + 1) * P], ident[:]
                    )

        def finish(u, half):
            if not tiles(u):
                return
            first, last = (u - u % 2, u - u % 2 + 1) if u < PAIRED_UNITS else (u, u)
            lo, hi = UNITS[first][0], UNITS[last][1]
            if first not in staged:
                staged[first] = keep.tile([P, CHUNKS, hi - lo], F32, name="staged_%d" % first)
            chunks = slice(2 * half, 2 * half + 2)
            for j in range(chunks.start, chunks.stop):
                nc.vector.scalar_tensor_tensor(
                    out=staged[first][:, j, UNITS[u][0] - lo : UNITS[u][1] - lo],
                    in0=z_t[u, j],
                    scalar=gain[:, j : j + 1],
                    in1=residual[u][:, j, :],
                    op0=ALU.mult,
                    op1=ALU.add,
                )
            if u == last:
                nc.sync.dma_start(
                    out=out_view[lo // N, :, chunks, lo % N : lo % N + hi - lo], in_=staged[first][:, chunks, :]
                )

        for g in range(PASSES):
            interleave(0, g, False)
        for s in range(WIDE_UNITS):
            statistics(s - 2)
            for g in range(PASSES):
                interleave(s + 1, g, False)
            interleave(s, 0, True)
            interleave(s, 1, True)
            quantise_and_multiply(s, 0)
            interleave(s, 2, True)
            add_bias(s - 1, 0)
            quantise_and_multiply(s, 1)
            add_bias(s - 1, 1)
            finish(s - 3, 0)
            normalise_on_vector(s - 2, 0)
            quantise_and_multiply(s, 2)
            normalise_on_vector(s - 2, 1)
            transpose(s - 2)
            finish(s - 3, 1)
            if s == 0:
                nc.scalar.copy(out=bias[:], in_=bias_ps[:])
                nc.scalar.copy(out=gain[:], in_=gain_ps[:])

        a, b = WIDE_UNITS, WIDE_UNITS + 1
        statistics(a - 2)
        for g in range(PASSES):
            interleave(b, g, False)
        for g in range(PASSES):
            quantise_and_multiply(a, g)
        add_bias(a - 1, 0)
        add_bias(a - 1, 1)
        finish(a - 3, 0)
        normalise_on_vector(a - 2, 0)
        normalise_on_vector(a - 2, 1)
        transpose(a - 2)
        finish(a - 3, 1)
        statistics(a - 1)
        for g in range(PASSES):
            quantise_and_multiply(b, g)
        add_bias(a, 0)
        finish(a - 2, 0)
        add_bias(b, 0)
        normalise_on_vector(a - 1, 0)
        normalise_on_vector(a - 1, 1)
        transpose(a - 1)
        finish(a - 2, 1)
        for u in (a, b):
            statistics(u)
            normalise_on_scalar(u)
        finish(a - 1, 0)
        finish(a - 1, 1)
        for u in (a, b):
            transpose(u)
            finish(u, 0)
            finish(u, 1)
